import numpy as np
import ml_dtypes


def mxq(x, axis, fmt="e4m3"):
    dtype, down = {"e4m3": (ml_dtypes.float8_e4m3fn, 7), "e5m2": (ml_dtypes.float8_e5m2, 14)}[fmt]
    v = np.moveaxis(np.asarray(x, np.float32).astype(ml_dtypes.bfloat16).astype(np.float64), axis, -1)
    blocks = v.reshape(v.shape[:-1] + (-1, 32))
    amax = np.abs(blocks).max(-1, keepdims=True)
    byte = np.maximum(np.where(amax > 0, np.frexp(amax)[1] - 1 + 127, 0) - down, 1)
    scale = np.exp2(byte - 127.0)
    codes = (blocks / scale).astype(np.float32).astype(dtype).astype(np.float64)
    return np.moveaxis((codes * scale).reshape(v.shape), -1, axis)


WIDE = False


def mx_kscale(k):
    if not WIDE:
        return np.ones(k)
    levels = np.array([10, -10, 5, -5, 0])
    a = np.random.permutation(np.resize(levels, k // 512 * 4)).reshape(k // 512, 4)
    idx = np.arange(k)
    return np.exp2(a[idx // 512, idx % 128 // 32])


BF16 = ml_dtypes.bfloat16


def bf(x):
    return np.asarray(x, np.float32).astype(BF16)


def f64(x):
    return np.asarray(x).astype(np.float64)


E2M1 = np.array([0.0, 0.5, 1.0, 1.5, 2.0, 3.0, 4.0, 6.0, -0.0, -0.5, -1.0, -1.5, -2.0, -3.0, -4.0, -6.0])


def pack_weight(w, fmt):
    k, n = w.shape
    w = f64(bf(w)).reshape(k // 32, 32, n)
    amax = np.abs(w).max(1)
    if fmt == "e4m3":
        byte = np.frexp(amax)[1] - 1 + 127 - 7
    else:
        mant, ex = np.frexp(amax / 6.0)
        byte = np.where(mant > 0.5, ex, ex - 1) + 127
    byte = np.clip(np.where(amax > 0, byte, 1), 1, 254)
    scaled = (w * np.exp2(127.0 - byte)[:, None, :]).reshape(k, n).astype(np.float32)
    by_word = np.ascontiguousarray(scaled.reshape(k // 512, 128, 4, n).transpose(0, 1, 3, 2))
    if fmt == "e4m3":
        words = by_word.astype(ml_dtypes.float8_e4m3fn).view(np.uint8)
    else:
        c = by_word.astype(ml_dtypes.float4_e2m1fn).view(np.uint8) & 0xF
        words = c[..., 0::2] | (c[..., 1::2] << 4)
    return np.ascontiguousarray(words), np.ascontiguousarray(byte.astype(np.uint8).reshape(k // 512, 16, n))


def unpack_weight(words, scales, fmt):
    g, p, n, _ = words.shape
    if fmt == "e4m3":
        vals = np.ascontiguousarray(words).view(ml_dtypes.float8_e4m3fn).astype(np.float64)
    else:
        nib = np.empty((g, p, n, 4), np.uint8)
        nib[..., 0::2] = words & 0xF
        nib[..., 1::2] = words >> 4
        vals = E2M1[nib]
    vals = vals * np.repeat(np.exp2(scales.astype(np.float64) - 127.0), 8, axis=1)[..., None]
    return vals.transpose(0, 1, 3, 2).reshape(g * 512, n)


N, G, GIN, GOUT = 128, 2, 4096, 3072

P0 = np.array([0.5, 1.0, 0.5, 0.3])
Q0 = np.array([0.5, 0.3, 0.2])


def rational(y, p, q):
    p = p[None, :, :, None]
    q = q[None, :, :, None]
    y2 = y * y
    y3 = y2 * y
    num = p[:, :, 0] + p[:, :, 1] * y + p[:, :, 2] * y2 + p[:, :, 3] * y3
    den = 1.0 + np.abs(q[:, :, 0] * y + q[:, :, 1] * y2 + q[:, :, 2] * y3)
    return num / den


def setup_inputs():
    s = mx_kscale(GIN)
    x = bf(np.random.standard_normal((N, G * GIN)) * np.tile(s, G))
    stack = np.random.standard_normal((G, GIN, GOUT)) / np.sqrt(GIN) / s[None, :, None]
    W_words, W_scales = pack_weight(stack.reshape(-1, GOUT), "e4m3")
    return {"x": x,
            "W_words": W_words,
            "W_scales": W_scales,
            "b": bf(np.random.standard_normal((G, GOUT)) * 0.3),
            "p": bf(P0 + 0.1 * np.random.standard_normal((G, P0.size))),
            "q": bf(Q0 + 0.05 * np.random.standard_normal((G, Q0.size)))}


def reference(x, W_words, W_scales, b, p, q):
    n = x.shape[0]
    xg = f64(x).reshape(n, G, GIN)
    xq = mxq(xg, 2, "e4m3")
    wq = unpack_weight(W_words, W_scales, "e4m3").reshape(G, GIN, GOUT)
    y = (xq.transpose(1, 0, 2) @ wq).transpose(1, 0, 2) + f64(b)[None]
    out = rational(y, f64(p), f64(q))
    return out.reshape(n, G * GOUT)

@@ -1,0 +1,235 @@
+from contextlib import ExitStack
+
+import concourse.mybir as mybir
+from concourse.masks import make_identity
+
+F32 = mybir.dt.float32
+BF16 = mybir.dt.bfloat16
+I32 = mybir.dt.int32
+U32 = mybir.dt.uint32
+U8 = mybir.dt.uint8
+FP8X4 = mybir.dt.float8_e4m3fn_x4
+ACT = mybir.ActivationFunctionType
+ALU = mybir.AluOpType
+
+P = 128
+PACK = 4
+K_PASS = P * PACK
+GROUPS = 2
+GIN = 4096
+GOUT = 3072
+GROUP_PASSES = GIN // K_PASS
+PASSES = GROUPS * GROUP_PASSES
+BANK = 512
+
+X_PIECES = 4
+PIECE_PASSES = PASSES // X_PIECES
+WORDS_PER_PASS = K_PASS // 2
+
+PLANES_PER_TILE = 4
+LOAD_PASSES = 4
+CHUNK = 1024
+PREFETCH = 3
+
+FLOPS = 2 * P * GIN * GOUT * GROUPS
+
+
+def column_chunks():
+    chunks = []
+    for grp in range(GROUPS):
+        for first in range(0, GOUT, CHUNK):
+            chunks.append((grp, first, CHUNK))
+    grp, first, width = chunks[-1]
+    half = width // 2
+    return chunks[:-1] + [(grp, first, half), (grp, first + half, half)]
+
+
+def tile_groupkanlayer_w_e_kernel(tc, x, W_words, W_scales, b, p, q, out):
+    nc = tc.nc
+    words_dram = W_words.rearrange("g p n t -> g p (n t)").bitcast(I32)
+    scales_dram = W_scales.bitcast(I32)
+
+    with ExitStack() as ctx:
+        consts = ctx.enter_context(tc.tile_pool(name="consts", bufs=1))
+        x_pool = ctx.enter_context(tc.tile_pool(name="x_pool", bufs=2))
+        w_pool = ctx.enter_context(tc.tile_pool(name="w_pool", bufs=2 * PREFETCH))
+        work = ctx.enter_context(tc.tile_pool(name="work", bufs=3))
+        setup_psum = ctx.enter_context(tc.psum_pool(name="setup_psum", bufs=4))
+        acc_psum = ctx.enter_context(tc.psum_pool(name="acc_psum", bufs=4))
+
+        x_codes = consts.tile([P, PASSES, P], U32, align_bytes=64)
+        x_planes = consts.tile([P, PASSES, P], U8, align_bytes=64)
+        w_planes = consts.tile([P, PASSES // PLANES_PER_TILE, GOUT], U8, align_bytes=64)
+        bias_all = consts.tile([P, GROUPS * GOUT], BF16)
+        bias_rows = consts.tile([P, BANK], BF16)
+        ident_f32 = consts.tile([P, P], F32)
+        ident_bf16 = consts.tile([P, P], BF16)
+        p_bf16 = consts.tile([P, GROUPS * 4], BF16)
+        q_bf16 = consts.tile([P, GROUPS * 3], BF16)
+        p_f32 = consts.tile([P, GROUPS * 4], F32)
+        q_f32 = consts.tile([P, GROUPS * 3], F32)
+
+        nc.vector.memset(w_planes[:].bitcast(I32), 0)
+        nc.vector.memset(bias_rows[:], 0.0)
+        make_identity(nc, ident_f32[:])
+        make_identity(nc, ident_bf16[:])
+
+        piece_cols = PIECE_PASSES * K_PASS
+        x_pieces = []
+        for i in range(X_PIECES):
+            x_piece = x_pool.tile([P, piece_cols], BF16, name="x_piece%d" % i, bufs=1)
+            nc.sync.dma_start(out=x_piece[:], in_=x[:, i * piece_cols : (i + 1) * piece_cols])
+            x_pieces.append(x_piece)
+
+        bias_blocks = GROUPS * GOUT // BANK
+        nc.scalar.dma_start(
+            out=bias_rows[0:bias_blocks, :], in_=b.rearrange("g (a c) -> (g a) c", c=BANK)
+        )
+        nc.scalar.dma_start(out=p_bf16[:], in_=p.rearrange("g c -> (g c)").partition_broadcast(P))
+        nc.scalar.dma_start(out=q_bf16[:], in_=q.rearrange("g c -> (g c)").partition_broadcast(P))
+        nc.vector.tensor_copy(out=p_f32[:], in_=p_bf16[:])
+        nc.vector.tensor_copy(out=q_f32[:], in_=q_bf16[:])
+
+        def load_scales(grp):
+            tiles_per_group = GROUP_PASSES // PLANES_PER_TILE
+            for j in range(grp * tiles_per_group, (grp + 1) * tiles_per_group):
+                for quad in range(4):
+                    nc.sync.dma_start(
+                        out=w_planes[32 * quad : 32 * quad + 16, j, :].bitcast(I32),
+                        in_=scales_dram[
+                            PLANES_PER_TILE * j : PLANES_PER_TILE * (j + 1),
+                            4 * quad : 4 * quad + 4,
+                            :,
+                        ],
+                    )
+
+        def load_weights(chunk):
+            grp, first, width = chunk
+            if first == 0:
+                load_scales(grp)
+            tiles = []
+            for h in range(GROUP_PASSES // LOAD_PASSES):
+                g0 = grp * GROUP_PASSES + h * LOAD_PASSES
+                w_codes = w_pool.tile([P, LOAD_PASSES, width], U32, tag="w_codes", align_bytes=64)
+                nc.sync.dma_start(
+                    out=w_codes[:].bitcast(I32),
+                    in_=words_dram[g0 : g0 + LOAD_PASSES, :, first : first + width].rearrange(
+                        "g p n -> p g n"
+                    ),
+                )
+                tiles.append(w_codes)
+            return tiles
+
+        chunks = column_chunks()
+        w_tiles = {}
+        for i in range(PREFETCH):
+            w_tiles[i] = load_weights(chunks[i])
+
+        for i in range(X_PIECES):
+            x_words = x_pieces[i][:].bitcast(F32)
+            grouped = x_pool.tile([P, PIECE_PASSES, P, PACK], BF16, align_bytes=64)
+            for half in range(2):
+                turned = setup_psum.tile([P, 2, 2, P], F32, tag="setup")
+                for g in range(2):
+                    w0 = (2 * half + g) * WORDS_PER_PASS
+                    for u in range(2):
+                        nc.tensor.transpose(
+                            turned[:, g, u, :],
+                            x_words[:, w0 + u : w0 + WORDS_PER_PASS : 2],
+                            ident_f32[:],
+                        )
+                copy = nc.vector.tensor_copy if half == 0 else nc.scalar.copy
+                copy(
+                    out=grouped[:, 2 * half : 2 * half + 2, :, :].bitcast(F32),
+                    in_=turned[:].rearrange("p g u n -> p g n u"),
+                )
+            passes = slice(i * PIECE_PASSES, (i + 1) * PIECE_PASSES)
+            nc.vector.quantize_mx(
+                out=x_codes[:, passes, :].rearrange("p g n -> p (g n)").bitcast(FP8X4),
+                scales=x_planes[:, passes, :].rearrange("p g n -> p (g n)"),
+                in_=grouped[:].rearrange("p g n t -> p (g n t)"),
+            )
+
+        for j in range(bias_blocks):
+            spread = setup_psum.tile([P, BANK], F32, tag="setup")
+            nc.tensor.matmul(
+                out=spread[:],
+                lhsT=ident_bf16[:, j : j + 1].to_broadcast([P, P]),
+                rhs=bias_rows[:],
+                start=True,
+                stop=True,
+            )
+            nc.scalar.copy(out=bias_all[:, j * BANK : (j + 1) * BANK], in_=spread[:])
+
+        for i, (grp, first, width) in enumerate(chunks):
+            half_width = width // 2
+            halves = [slice(h * half_width, (h + 1) * half_width) for h in range(2)]
+
+            sums = []
+            for h in range(2):
+                sums.append(acc_psum.tile([P, half_width], F32, tag="sums", name="sums%d" % h))
+            for g_local in range(GROUP_PASSES):
+                g = grp * GROUP_PASSES + g_local
+                w_codes = w_tiles[i][g_local // LOAD_PASSES]
+                offset = 4 * (g % PLANES_PER_TILE)
+                for h in range(2):
+                    nc.tensor.matmul_mx(
+                        out=sums[h][:],
+                        lhsT=x_codes[:, g, :].bitcast(FP8X4),
+                        lhsT_scale=x_planes[:, g, :],
+                        rhs=w_codes[:, g_local % LOAD_PASSES, halves[h]].bitcast(FP8X4),
+                        rhs_scale=w_planes[
+                            offset:P,
+                            g // PLANES_PER_TILE,
+                            first + h * half_width : first + (h + 1) * half_width,
+                        ],
+                        start=(g_local == 0),
+                        stop=(g_local == GROUP_PASSES - 1),
+                    )
+
+            if i + PREFETCH < len(chunks):
+                w_tiles[i + PREFETCH] = load_weights(chunks[i + PREFETCH])
+
+            p0, p1, p2, p3 = [p_f32[:, 4 * grp + c : 4 * grp + c + 1] for c in range(4)]
+            q0, q1, q2 = [q_f32[:, 3 * grp + c : 3 * grp + c + 1] for c in range(3)]
+            out_first = grp * GOUT + first
+
+            y = work.tile([P, width], F32)
+            num = work.tile([P, width], F32)
+            den = work.tile([P, width], F32)
+            for h in range(2):
+                nc.vector.tensor_tensor(
+                    out=y[:, halves[h]],
+                    in0=sums[h][:],
+                    in1=bias_all[:, out_first + h * half_width : out_first + (h + 1) * half_width],
+                    op=ALU.add,
+                )
+            for s in halves:
+                nc.scalar.activation(out=den[:, s], in_=y[:, s], func=ACT.Identity, scale=q2, bias=q1)
+            for s in halves:
+                nc.scalar.activation(out=num[:, s], in_=y[:, s], func=ACT.Identity, scale=p3, bias=p2)
+            for s in halves:
+                nc.vector.tensor_tensor(out=den[:, s], in0=den[:, s], in1=y[:, s], op=ALU.mult)
+            for s in halves:
+                nc.vector.scalar_tensor_tensor(
+                    out=den[:, s], in0=den[:, s], scalar=q0, in1=y[:, s], op0=ALU.add, op1=ALU.mult
+                )
+            for s in halves:
+                nc.scalar.activation(out=den[:, s], in_=den[:, s], func=ACT.Abs)
+            for s in halves:
+                nc.scalar.activation(
+                    out=den[:, s], in_=den[:, s], func=ACT.Abs_reciprocal_sqrt, bias=1.0
+                )
+            for s in halves:
+                nc.scalar.activation(out=den[:, s], in_=den[:, s], func=ACT.Square)
+            for s in halves:
+                nc.vector.tensor_tensor(out=num[:, s], in0=num[:, s], in1=y[:, s], op=ALU.mult)
+            for s in halves:
+                nc.vector.scalar_tensor_tensor(
+                    out=num[:, s], in0=num[:, s], scalar=p1, in1=y[:, s], op0=ALU.add, op1=ALU.mult
+                )
+            for s in halves:
+                nc.vector.scalar_tensor_tensor(
+                    out=num[:, s], in0=num[:, s], scalar=p0, in1=den[:, s], op0=ALU.add, op1=ALU.mult
+                )
+            nc.sync.dma_start(out=out[:, out_first : out_first + width], in_=num[:])

@@ -50,10 +50,11 @@ def tile_groupkanlayer_w_e_kernel(tc, x, W_words, W_scales, b, p, q, out):
     scales_dram = W_scales.bitcast(I32)
 
     with ExitStack() as ctx:
+        ctx.enter_context(tc.manual_schedule())
         consts = ctx.enter_context(tc.tile_pool(name="consts", bufs=1))
         x_pool = ctx.enter_context(tc.tile_pool(name="x_pool", bufs=2))
         w_pool = ctx.enter_context(tc.tile_pool(name="w_pool", bufs=2 * PREFETCH))
-        work = ctx.enter_context(tc.tile_pool(name="work", bufs=3))
+        work = ctx.enter_context(tc.tile_pool(name="work", bufs=2))
         setup_psum = ctx.enter_context(tc.psum_pool(name="setup_psum", bufs=4))
         acc_psum = ctx.enter_context(tc.psum_pool(name="acc_psum", bufs=4))
 
@@ -62,6 +63,7 @@ def tile_groupkanlayer_w_e_kernel(tc, x, W_words, W_scales, b, p, q, out):
         w_planes = consts.tile([P, PASSES // PLANES_PER_TILE, GOUT], U8, align_bytes=64)
         bias_all = consts.tile([P, GROUPS * GOUT], BF16)
         bias_rows = consts.tile([P, BANK], BF16)
+        result = consts.tile([P, GROUPS * GOUT], F32)
         ident_f32 = consts.tile([P, P], F32)
         ident_bf16 = consts.tile([P, P], BF16)
         p_bf16 = consts.tile([P, GROUPS * 4], BF16)
@@ -87,8 +89,6 @@ def tile_groupkanlayer_w_e_kernel(tc, x, W_words, W_scales, b, p, q, out):
         )
         nc.scalar.dma_start(out=p_bf16[:], in_=p.rearrange("g c -> (g c)").partition_broadcast(P))
         nc.scalar.dma_start(out=q_bf16[:], in_=q.rearrange("g c -> (g c)").partition_broadcast(P))
-        nc.vector.tensor_copy(out=p_f32[:], in_=p_bf16[:])
-        nc.vector.tensor_copy(out=q_f32[:], in_=q_bf16[:])
 
         def load_scales(grp):
             tiles_per_group = GROUP_PASSES // PLANES_PER_TILE
@@ -125,9 +125,19 @@ def tile_groupkanlayer_w_e_kernel(tc, x, W_words, W_scales, b, p, q, out):
         for i in range(PREFETCH):
             w_tiles[i] = load_weights(chunks[i])
 
+        def quantise_piece(i, grouped):
+            passes = slice(i * PIECE_PASSES, (i + 1) * PIECE_PASSES)
+            nc.vector.quantize_mx(
+                out=x_codes[:, passes, :].rearrange("p g n -> p (g n)").bitcast(FP8X4),
+                scales=x_planes[:, passes, :].rearrange("p g n -> p (g n)"),
+                in_=grouped[:].rearrange("p g n t -> p (g n t)"),
+            )
+
+        regrouped = []
         for i in range(X_PIECES):
             x_words = x_pieces[i][:].bitcast(F32)
             grouped = x_pool.tile([P, PIECE_PASSES, P, PACK], BF16, align_bytes=64)
+            regrouped.append(grouped)
             for half in range(2):
                 turned = setup_psum.tile([P, 2, 2, P], F32, tag="setup")
                 for g in range(2):
@@ -143,12 +153,9 @@ def tile_groupkanlayer_w_e_kernel(tc, x, W_words, W_scales, b, p, q, out):
                     out=grouped[:, 2 * half : 2 * half + 2, :, :].bitcast(F32),
                     in_=turned[:].rearrange("p g u n -> p g n u"),
                 )
-            passes = slice(i * PIECE_PASSES, (i + 1) * PIECE_PASSES)
-            nc.vector.quantize_mx(
-                out=x_codes[:, passes, :].rearrange("p g n -> p (g n)").bitcast(FP8X4),
-                scales=x_planes[:, passes, :].rearrange("p g n -> p (g n)"),
-                in_=grouped[:].rearrange("p g n t -> p (g n t)"),
-            )
+            if i > 0:
+                quantise_piece(i - 1, regrouped[i - 1])
+        quantise_piece(X_PIECES - 1, regrouped[X_PIECES - 1])
 
         for j in range(bias_blocks):
             spread = setup_psum.tile([P, BANK], F32, tag="setup")
@@ -159,7 +166,11 @@ def tile_groupkanlayer_w_e_kernel(tc, x, W_words, W_scales, b, p, q, out):
                 start=True,
                 stop=True,
             )
-            nc.scalar.copy(out=bias_all[:, j * BANK : (j + 1) * BANK], in_=spread[:])
+            copy = nc.vector.tensor_copy if j % 2 == 0 else nc.scalar.copy
+            copy(out=bias_all[:, j * BANK : (j + 1) * BANK], in_=spread[:])
+
+        nc.vector.tensor_copy(out=p_f32[:], in_=p_bf16[:])
+        nc.vector.tensor_copy(out=q_f32[:], in_=q_bf16[:])
 
         for i, (grp, first, width) in enumerate(chunks):
             half_width = width // 2
@@ -228,8 +239,16 @@ def tile_groupkanlayer_w_e_kernel(tc, x, W_words, W_scales, b, p, q, out):
                 nc.vector.scalar_tensor_tensor(
                     out=num[:, s], in0=num[:, s], scalar=p1, in1=y[:, s], op0=ALU.add, op1=ALU.mult
                 )
-            for s in halves:
+            for h in range(2):
                 nc.vector.scalar_tensor_tensor(
-                    out=num[:, s], in0=num[:, s], scalar=p0, in1=den[:, s], op0=ALU.add, op1=ALU.mult
+                    out=result[:, out_first + h * half_width : out_first + (h + 1) * half_width],
+                    in0=num[:, halves[h]],
+                    scalar=p0,
+                    in1=den[:, halves[h]],
+                    op0=ALU.add,
+                    op1=ALU.mult,
                 )
-            nc.sync.dma_start(out=out[:, out_first : out_first + width], in_=num[:])
+
+        for grp, first, width in chunks:
+            cols = slice(grp * GOUT + first, grp * GOUT + first + width)
+            nc.sync.dma_start(out=out[:, cols], in_=result[:, cols])

@@ -27,33 +27,37 @@ PIECE_PASSES = PASSES // X_PIECES
 WORDS_PER_PASS = K_PASS // 2
 
 PLANES_PER_TILE = 4
-LOAD_PASSES = 4
+LOAD_PASSES = 2
 CHUNK = 1024
+NARROW_CHUNK = 512
+NARROW_COLUMNS = 2048
 PREFETCH = 3
 
 FLOPS = 2 * P * GIN * GOUT * GROUPS
 
 
 def column_chunks():
+    wide_columns = GROUPS * GOUT - NARROW_COLUMNS
     chunks = []
-    for grp in range(GROUPS):
-        for first in range(0, GOUT, CHUNK):
-            chunks.append((grp, first, CHUNK))
-    grp, first, width = chunks[-1]
-    half = width // 2
-    return chunks[:-1] + [(grp, first, half), (grp, first + half, half)]
+    for column in range(0, wide_columns, CHUNK):
+        chunks.append((column // GOUT, column % GOUT, CHUNK))
+    for column in range(wide_columns, GROUPS * GOUT, NARROW_CHUNK):
+        chunks.append((column // GOUT, column % GOUT, NARROW_CHUNK))
+    return chunks
 
 
 def tile_groupkanlayer_w_e_kernel(tc, x, W_words, W_scales, b, p, q, out):
     nc = tc.nc
     words_dram = W_words.rearrange("g p n t -> g p (n t)").bitcast(I32)
-    scales_dram = W_scales.bitcast(I32)
+    scales_dram = W_scales.bitcast(F32)
 
     with ExitStack() as ctx:
         ctx.enter_context(tc.manual_schedule())
         consts = ctx.enter_context(tc.tile_pool(name="consts", bufs=1))
         x_pool = ctx.enter_context(tc.tile_pool(name="x_pool", bufs=2))
-        w_pool = ctx.enter_context(tc.tile_pool(name="w_pool", bufs=2 * PREFETCH))
+        w_pool = ctx.enter_context(
+            tc.tile_pool(name="w_pool", bufs=PREFETCH * GROUP_PASSES // LOAD_PASSES)
+        )
         work = ctx.enter_context(tc.tile_pool(name="work", bufs=2))
         setup_psum = ctx.enter_context(tc.psum_pool(name="setup_psum", bufs=4))
         acc_psum = ctx.enter_context(tc.psum_pool(name="acc_psum", bufs=4))
@@ -90,23 +94,17 @@ def tile_groupkanlayer_w_e_kernel(tc, x, W_words, W_scales, b, p, q, out):
         nc.scalar.dma_start(out=p_bf16[:], in_=p.rearrange("g c -> (g c)").partition_broadcast(P))
         nc.scalar.dma_start(out=q_bf16[:], in_=q.rearrange("g c -> (g c)").partition_broadcast(P))
 
-        def load_scales(grp):
-            tiles_per_group = GROUP_PASSES // PLANES_PER_TILE
-            for j in range(grp * tiles_per_group, (grp + 1) * tiles_per_group):
-                for quad in range(4):
-                    nc.sync.dma_start(
-                        out=w_planes[32 * quad : 32 * quad + 16, j, :].bitcast(I32),
-                        in_=scales_dram[
-                            PLANES_PER_TILE * j : PLANES_PER_TILE * (j + 1),
-                            4 * quad : 4 * quad + 4,
-                            :,
-                        ],
-                    )
+        for j in range(PASSES // PLANES_PER_TILE):
+            for quad in range(4):
+                nc.gpsimd.dma_start(
+                    out=w_planes[32 * quad : 32 * quad + 16, j, :].bitcast(F32),
+                    in_=scales_dram[
+                        PLANES_PER_TILE * j : PLANES_PER_TILE * (j + 1), 4 * quad : 4 * quad + 4, :
+                    ],
+                )
 
         def load_weights(chunk):
             grp, first, width = chunk
-            if first == 0:
-                load_scales(grp)
             tiles = []
             for h in range(GROUP_PASSES // LOAD_PASSES):
                 g0 = grp * GROUP_PASSES + h * LOAD_PASSES
@@ -172,13 +170,14 @@ def tile_groupkanlayer_w_e_kernel(tc, x, W_words, W_scales, b, p, q, out):
         nc.vector.tensor_copy(out=p_f32[:], in_=p_bf16[:])
         nc.vector.tensor_copy(out=q_f32[:], in_=q_bf16[:])
 
-        for i, (grp, first, width) in enumerate(chunks):
-            half_width = width // 2
-            halves = [slice(h * half_width, (h + 1) * half_width) for h in range(2)]
+        def half_slices(width, first=0):
+            return [slice(first + h * (width // 2), first + (h + 1) * (width // 2)) for h in range(2)]
 
+        def multiply(i):
+            grp, first, width = chunks[i]
             sums = []
             for h in range(2):
-                sums.append(acc_psum.tile([P, half_width], F32, tag="sums", name="sums%d" % h))
+                sums.append(acc_psum.tile([P, width // 2], F32, tag="sums", name="sums%d" % h))
             for g_local in range(GROUP_PASSES):
                 g = grp * GROUP_PASSES + g_local
                 w_codes = w_tiles[i][g_local // LOAD_PASSES]
@@ -188,37 +187,41 @@ def tile_groupkanlayer_w_e_kernel(tc, x, W_words, W_scales, b, p, q, out):
                         out=sums[h][:],
                         lhsT=x_codes[:, g, :].bitcast(FP8X4),
                         lhsT_scale=x_planes[:, g, :],
-                        rhs=w_codes[:, g_local % LOAD_PASSES, halves[h]].bitcast(FP8X4),
-                        rhs_scale=w_planes[
-                            offset:P,
-                            g // PLANES_PER_TILE,
-                            first + h * half_width : first + (h + 1) * half_width,
-                        ],
+                        rhs=w_codes[:, g_local % LOAD_PASSES, half_slices(width)[h]].bitcast(FP8X4),
+                        rhs_scale=w_planes[offset:P, g // PLANES_PER_TILE, half_slices(width, first)[h]],
                         start=(g_local == 0),
                         stop=(g_local == GROUP_PASSES - 1),
                     )
+            return sums
 
-            if i + PREFETCH < len(chunks):
-                w_tiles[i + PREFETCH] = load_weights(chunks[i + PREFETCH])
+        def coefficients(grp):
+            return (
+                [p_f32[:, 4 * grp + c : 4 * grp + c + 1] for c in range(4)],
+                [q_f32[:, 3 * grp + c : 3 * grp + c + 1] for c in range(3)],
+            )
 
-            p0, p1, p2, p3 = [p_f32[:, 4 * grp + c : 4 * grp + c + 1] for c in range(4)]
-            q0, q1, q2 = [q_f32[:, 3 * grp + c : 3 * grp + c + 1] for c in range(3)]
-            out_first = grp * GOUT + first
-
+        def begin_rational(i, sums):
+            grp, first, width = chunks[i]
+            (p0, p1, p2, p3), (q0, q1, q2) = coefficients(grp)
             y = work.tile([P, width], F32)
             num = work.tile([P, width], F32)
             den = work.tile([P, width], F32)
+            halves = half_slices(width)
+            out_halves = half_slices(width, grp * GOUT + first)
             for h in range(2):
                 nc.vector.tensor_tensor(
-                    out=y[:, halves[h]],
-                    in0=sums[h][:],
-                    in1=bias_all[:, out_first + h * half_width : out_first + (h + 1) * half_width],
-                    op=ALU.add,
+                    out=y[:, halves[h]], in0=sums[h][:], in1=bias_all[:, out_halves[h]], op=ALU.add
                 )
             for s in halves:
                 nc.scalar.activation(out=den[:, s], in_=y[:, s], func=ACT.Identity, scale=q2, bias=q1)
             for s in halves:
                 nc.scalar.activation(out=num[:, s], in_=y[:, s], func=ACT.Identity, scale=p3, bias=p2)
+            return y, num, den
+
+        def continue_rational(i, y, num, den):
+            grp, first, width = chunks[i]
+            (p0, p1, p2, p3), (q0, q1, q2) = coefficients(grp)
+            halves = half_slices(width)
             for s in halves:
                 nc.vector.tensor_tensor(out=den[:, s], in0=den[:, s], in1=y[:, s], op=ALU.mult)
             for s in halves:
@@ -239,15 +242,33 @@ def tile_groupkanlayer_w_e_kernel(tc, x, W_words, W_scales, b, p, q, out):
                 nc.vector.scalar_tensor_tensor(
                     out=num[:, s], in0=num[:, s], scalar=p1, in1=y[:, s], op0=ALU.add, op1=ALU.mult
                 )
+
+        def finish_rational(i, num, den):
+            grp, first, width = chunks[i]
+            (p0, p1, p2, p3), (q0, q1, q2) = coefficients(grp)
+            halves = half_slices(width)
+            out_halves = half_slices(width, grp * GOUT + first)
             for h in range(2):
                 nc.vector.scalar_tensor_tensor(
-                    out=result[:, out_first + h * half_width : out_first + (h + 1) * half_width],
+                    out=result[:, out_halves[h]],
                     in0=num[:, halves[h]],
                     scalar=p0,
                     in1=den[:, halves[h]],
                     op0=ALU.add,
                     op1=ALU.mult,
                 )
+
+        waiting = None
+        for i in range(len(chunks)):
+            sums = multiply(i)
+            if i + PREFETCH < len(chunks):
+                w_tiles[i + PREFETCH] = load_weights(chunks[i + PREFETCH])
+            y, num, den = begin_rational(i, sums)
+            if waiting is not None:
+                finish_rational(*waiting)
+            continue_rational(i, y, num, den)
+            waiting = (i, num, den)
+        finish_rational(*waiting)
 
         for grp, first, width in chunks:
             cols = slice(grp * GOUT + first, grp * GOUT + first + width)

@@ -49,7 +49,7 @@ def column_chunks():
 def tile_groupkanlayer_w_e_kernel(tc, x, W_words, W_scales, b, p, q, out):
     nc = tc.nc
     words_dram = W_words.rearrange("g p n t -> g p (n t)").bitcast(I32)
-    scales_dram = W_scales.bitcast(F32)
+    scales_dram = W_scales.bitcast(I32)
 
     with ExitStack() as ctx:
         ctx.enter_context(tc.manual_schedule())
@@ -96,8 +96,8 @@ def tile_groupkanlayer_w_e_kernel(tc, x, W_words, W_scales, b, p, q, out):
 
         for j in range(PASSES // PLANES_PER_TILE):
             for quad in range(4):
-                nc.gpsimd.dma_start(
-                    out=w_planes[32 * quad : 32 * quad + 16, j, :].bitcast(F32),
+                nc.sync.dma_start(
+                    out=w_planes[32 * quad : 32 * quad + 16, j, :].bitcast(I32),
                     in_=scales_dram[
                         PLANES_PER_TILE * j : PLANES_PER_TILE * (j + 1), 4 * quad : 4 * quad + 4, :
                     ],

@@ -49,7 +49,7 @@ def column_chunks():
 def tile_groupkanlayer_w_e_kernel(tc, x, W_words, W_scales, b, p, q, out):
     nc = tc.nc
     words_dram = W_words.rearrange("g p n t -> g p (n t)").bitcast(I32)
-    scales_dram = W_scales.bitcast(I32)
+    scales_dram = W_scales.bitcast(F32)
 
     with ExitStack() as ctx:
         ctx.enter_context(tc.manual_schedule())
@@ -75,8 +75,8 @@ def tile_groupkanlayer_w_e_kernel(tc, x, W_words, W_scales, b, p, q, out):
         p_f32 = consts.tile([P, GROUPS * 4], F32)
         q_f32 = consts.tile([P, GROUPS * 3], F32)
 
-        nc.vector.memset(w_planes[:].bitcast(I32), 0)
         nc.vector.memset(bias_rows[:], 0.0)
+        nc.vector.memset(w_planes[:].bitcast(I32), 0)
         make_identity(nc, ident_f32[:])
         make_identity(nc, ident_bf16[:])
 
@@ -96,8 +96,8 @@ def tile_groupkanlayer_w_e_kernel(tc, x, W_words, W_scales, b, p, q, out):
 
         for j in range(PASSES // PLANES_PER_TILE):
             for quad in range(4):
-                nc.sync.dma_start(
-                    out=w_planes[32 * quad : 32 * quad + 16, j, :].bitcast(I32),
+                nc.gpsimd.dma_start(
+                    out=w_planes[32 * quad : 32 * quad + 16, j, :].bitcast(F32),
                     in_=scales_dram[
                         PLANES_PER_TILE * j : PLANES_PER_TILE * (j + 1), 4 * quad : 4 * quad + 4, :
                     ],
@@ -131,6 +131,19 @@ def tile_groupkanlayer_w_e_kernel(tc, x, W_words, W_scales, b, p, q, out):
                 in_=grouped[:].rearrange("p g n t -> p (g n t)"),
             )
 
+        def spread_bias(j):
+            spread = setup_psum.tile([P, BANK], F32, tag="setup")
+            nc.tensor.matmul(
+                out=spread[:],
+                lhsT=ident_bf16[:, j : j + 1].to_broadcast([P, P]),
+                rhs=bias_rows[:],
+                start=True,
+                stop=True,
+            )
+            copy = nc.vector.tensor_copy if j % 2 == 0 else nc.scalar.copy
+            copy(out=bias_all[:, j * BANK : (j + 1) * BANK], in_=spread[:])
+
+        piece_blocks = bias_blocks // X_PIECES
         regrouped = []
         for i in range(X_PIECES):
             x_words = x_pieces[i][:].bitcast(F32)
@@ -153,19 +166,9 @@ def tile_groupkanlayer_w_e_kernel(tc, x, W_words, W_scales, b, p, q, out):
                 )
             if i > 0:
                 quantise_piece(i - 1, regrouped[i - 1])
+            for j in range(i * piece_blocks, (i + 1) * piece_blocks):
+                spread_bias(j)
         quantise_piece(X_PIECES - 1, regrouped[X_PIECES - 1])
-
-        for j in range(bias_blocks):
-            spread = setup_psum.tile([P, BANK], F32, tag="setup")
-            nc.tensor.matmul(
-                out=spread[:],
-                lhsT=ident_bf16[:, j : j + 1].to_broadcast([P, P]),
-                rhs=bias_rows[:],
-                start=True,
-                stop=True,
-            )
-            copy = nc.vector.tensor_copy if j % 2 == 0 else nc.scalar.copy
-            copy(out=bias_all[:, j * BANK : (j + 1) * BANK], in_=spread[:])
 
         nc.vector.tensor_copy(out=p_f32[:], in_=p_bf16[:])
         nc.vector.tensor_copy(out=q_f32[:], in_=q_bf16[:])

@@ -32,6 +32,8 @@ CHUNK = 1024
 NARROW_CHUNK = 512
 NARROW_COLUMNS = 2048
 PREFETCH = 3
+Q_COLUMN = 16
+PQ_COLUMNS = 32
 
 FLOPS = 2 * P * GIN * GOUT * GROUPS
 
@@ -70,10 +72,7 @@ def tile_groupkanlayer_w_e_kernel(tc, x, W_words, W_scales, b, p, q, out):
         result = consts.tile([P, GROUPS * GOUT], F32)
         ident_f32 = consts.tile([P, P], F32)
         ident_bf16 = consts.tile([P, P], BF16)
-        p_bf16 = consts.tile([P, GROUPS * 4], BF16)
-        q_bf16 = consts.tile([P, GROUPS * 3], BF16)
-        p_f32 = consts.tile([P, GROUPS * 4], F32)
-        q_f32 = consts.tile([P, GROUPS * 3], F32)
+        pq_f32 = consts.tile([P, GROUPS, PQ_COLUMNS], F32)
 
         nc.vector.memset(bias_rows[:], 0.0)
         nc.vector.memset(w_planes[:].bitcast(I32), 0)
@@ -91,8 +90,10 @@ def tile_groupkanlayer_w_e_kernel(tc, x, W_words, W_scales, b, p, q, out):
         nc.scalar.dma_start(
             out=bias_rows[0:bias_blocks, :], in_=b.rearrange("g (a c) -> (g a) c", c=BANK)
         )
-        nc.scalar.dma_start(out=p_bf16[:], in_=p.rearrange("g c -> (g c)").partition_broadcast(P))
-        nc.scalar.dma_start(out=q_bf16[:], in_=q.rearrange("g c -> (g c)").partition_broadcast(P))
+        nc.scalar.dma_start(out=bias_rows[bias_blocks : bias_blocks + GROUPS, 0:4], in_=p)
+        nc.scalar.dma_start(
+            out=bias_rows[bias_blocks : bias_blocks + GROUPS, Q_COLUMN : Q_COLUMN + 3], in_=q
+        )
 
         for j in range(PASSES // PLANES_PER_TILE):
             for quad in range(4):
@@ -143,6 +144,18 @@ def tile_groupkanlayer_w_e_kernel(tc, x, W_words, W_scales, b, p, q, out):
             copy = nc.vector.tensor_copy if j % 2 == 0 else nc.scalar.copy
             copy(out=bias_all[:, j * BANK : (j + 1) * BANK], in_=spread[:])
 
+        def spread_coefficients():
+            spread = setup_psum.tile([P, GROUPS, PQ_COLUMNS], F32, tag="setup")
+            for grp in range(GROUPS):
+                nc.tensor.matmul(
+                    out=spread[:, grp, :],
+                    lhsT=ident_bf16[:, bias_blocks + grp : bias_blocks + grp + 1].to_broadcast([P, P]),
+                    rhs=bias_rows[:, 0:PQ_COLUMNS],
+                    start=True,
+                    stop=True,
+                )
+            nc.vector.tensor_copy(out=pq_f32[:], in_=spread[:])
+
         piece_blocks = bias_blocks // X_PIECES
         regrouped = []
         for i in range(X_PIECES):
@@ -170,8 +183,7 @@ def tile_groupkanlayer_w_e_kernel(tc, x, W_words, W_scales, b, p, q, out):
                 spread_bias(j)
         quantise_piece(X_PIECES - 1, regrouped[X_PIECES - 1])
 
-        nc.vector.tensor_copy(out=p_f32[:], in_=p_bf16[:])
-        nc.vector.tensor_copy(out=q_f32[:], in_=q_bf16[:])
+        spread_coefficients()
 
         def half_slices(width, first=0):
             return [slice(first + h * (width // 2), first + (h + 1) * (width // 2)) for h in range(2)]
@@ -199,8 +211,8 @@ def tile_groupkanlayer_w_e_kernel(tc, x, W_words, W_scales, b, p, q, out):
 
         def coefficients(grp):
             return (
-                [p_f32[:, 4 * grp + c : 4 * grp + c + 1] for c in range(4)],
-                [q_f32[:, 3 * grp + c : 3 * grp + c + 1] for c in range(3)],
+                [pq_f32[:, grp, c : c + 1] for c in range(4)],
+                [pq_f32[:, grp, Q_COLUMN + c : Q_COLUMN + c + 1] for c in range(3)],
             )
 
         def begin_rational(i, sums):

@@ -27,7 +27,7 @@ PIECE_PASSES = PASSES // X_PIECES
 WORDS_PER_PASS = K_PASS // 2
 
 PLANES_PER_TILE = 4
-LOAD_PASSES = 2
+LOADS = (2, 2, 2, 1, 1)
 CHUNK = 1024
 NARROW_CHUNK = 512
 NARROW_COLUMNS = 2048
@@ -57,9 +57,7 @@ def tile_groupkanlayer_w_e_kernel(tc, x, W_words, W_scales, b, p, q, out):
         ctx.enter_context(tc.manual_schedule())
         consts = ctx.enter_context(tc.tile_pool(name="consts", bufs=1))
         x_pool = ctx.enter_context(tc.tile_pool(name="x_pool", bufs=2))
-        w_pool = ctx.enter_context(
-            tc.tile_pool(name="w_pool", bufs=PREFETCH * GROUP_PASSES // LOAD_PASSES)
-        )
+        w_pool = ctx.enter_context(tc.tile_pool(name="w_pool", bufs=PREFETCH))
         work = ctx.enter_context(tc.tile_pool(name="work", bufs=2))
         setup_psum = ctx.enter_context(tc.psum_pool(name="setup_psum", bufs=4))
         acc_psum = ctx.enter_context(tc.psum_pool(name="acc_psum", bufs=4))
@@ -106,18 +104,26 @@ def tile_groupkanlayer_w_e_kernel(tc, x, W_words, W_scales, b, p, q, out):
 
         def load_weights(chunk):
             grp, first, width = chunk
-            tiles = []
-            for h in range(GROUP_PASSES // LOAD_PASSES):
-                g0 = grp * GROUP_PASSES + h * LOAD_PASSES
-                w_codes = w_pool.tile([P, LOAD_PASSES, width], U32, tag="w_codes", align_bytes=64)
+            by_pass = []
+            g0 = grp * GROUP_PASSES
+            for passes in LOADS:
+                w_codes = w_pool.tile(
+                    [P, passes, width],
+                    U32,
+                    tag="w_codes%d" % passes,
+                    bufs=PREFETCH * sum(1 for n in LOADS if n == passes),
+                    align_bytes=64,
+                )
                 nc.sync.dma_start(
                     out=w_codes[:].bitcast(I32),
-                    in_=words_dram[g0 : g0 + LOAD_PASSES, :, first : first + width].rearrange(
+                    in_=words_dram[g0 : g0 + passes, :, first : first + width].rearrange(
                         "g p n -> p g n"
                     ),
                 )
-                tiles.append(w_codes)
-            return tiles
+                for k in range(passes):
+                    by_pass.append((w_codes, k))
+                g0 += passes
+            return by_pass
 
         chunks = column_chunks()
         w_tiles = {}
@@ -195,14 +201,14 @@ def tile_groupkanlayer_w_e_kernel(tc, x, W_words, W_scales, b, p, q, out):
                 sums.append(acc_psum.tile([P, width // 2], F32, tag="sums", name="sums%d" % h))
             for g_local in range(GROUP_PASSES):
                 g = grp * GROUP_PASSES + g_local
-                w_codes = w_tiles[i][g_local // LOAD_PASSES]
+                w_codes, place = w_tiles[i][g_local]
                 offset = 4 * (g % PLANES_PER_TILE)
                 for h in range(2):
                     nc.tensor.matmul_mx(
                         out=sums[h][:],
                         lhsT=x_codes[:, g, :].bitcast(FP8X4),
                         lhsT_scale=x_planes[:, g, :],
-                        rhs=w_codes[:, g_local % LOAD_PASSES, half_slices(width)[h]].bitcast(FP8X4),
+                        rhs=w_codes[:, place, half_slices(width)[h]].bitcast(FP8X4),
                         rhs_scale=w_planes[offset:P, g // PLANES_PER_TILE, half_slices(width, first)[h]],
                         start=(g_local == 0),
                         stop=(g_local == GROUP_PASSES - 1),

from contextlib import ExitStack

import concourse.mybir as mybir
from concourse.masks import make_identity

F32 = mybir.dt.float32
BF16 = mybir.dt.bfloat16
I32 = mybir.dt.int32
U32 = mybir.dt.uint32
U8 = mybir.dt.uint8
FP8X4 = mybir.dt.float8_e4m3fn_x4
ACT = mybir.ActivationFunctionType
ALU = mybir.AluOpType

P = 128
PACK = 4
K_PASS = P * PACK
GROUPS = 2
GIN = 4096
GOUT = 3072
GROUP_PASSES = GIN // K_PASS
PASSES = GROUPS * GROUP_PASSES
BANK = 512

X_PIECES = 4
PIECE_PASSES = PASSES // X_PIECES
WORDS_PER_PASS = K_PASS // 2

PLANES_PER_TILE = 4
LOADS = (2, 2, 2, 1, 1)
CHUNK = 1024
NARROW_CHUNK = 512
NARROW_COLUMNS = 2048
PREFETCH = 3
Q_COLUMN = 16
PQ_COLUMNS = 32

FLOPS = 2 * P * GIN * GOUT * GROUPS


def column_chunks():
    wide_columns = GROUPS * GOUT - NARROW_COLUMNS
    chunks = []
    for column in range(0, wide_columns, CHUNK):
        chunks.append((column // GOUT, column % GOUT, CHUNK))
    for column in range(wide_columns, GROUPS * GOUT, NARROW_CHUNK):
        chunks.append((column // GOUT, column % GOUT, NARROW_CHUNK))
    return chunks


def tile_groupkanlayer_w_e_kernel(tc, x, W_words, W_scales, b, p, q, out):
    nc = tc.nc
    words_dram = W_words.rearrange("g p n t -> g p (n t)").bitcast(I32)
    scales_dram = W_scales.bitcast(F32)

    with ExitStack() as ctx:
        ctx.enter_context(tc.manual_schedule())
        consts = ctx.enter_context(tc.tile_pool(name="consts", bufs=1))
        x_pool = ctx.enter_context(tc.tile_pool(name="x_pool", bufs=2))
        w_pool = ctx.enter_context(tc.tile_pool(name="w_pool", bufs=PREFETCH))
        work = ctx.enter_context(tc.tile_pool(name="work", bufs=2))
        setup_psum = ctx.enter_context(tc.psum_pool(name="setup_psum", bufs=4))
        acc_psum = ctx.enter_context(tc.psum_pool(name="acc_psum", bufs=4))

        x_codes = consts.tile([P, PASSES, P], U32, align_bytes=64)
        x_planes = consts.tile([P, PASSES, P], U8, align_bytes=64)
        w_planes = consts.tile([P, PASSES // PLANES_PER_TILE, GOUT], U8, align_bytes=64)
        bias_all = consts.tile([P, GROUPS * GOUT], BF16)
        bias_rows = consts.tile([P, BANK], BF16)
        result = consts.tile([P, GROUPS * GOUT], F32)
        ident_f32 = consts.tile([P, P], F32)
        ident_bf16 = consts.tile([P, P], BF16)
        pq_f32 = consts.tile([P, GROUPS, PQ_COLUMNS], F32)

        nc.vector.memset(bias_rows[:], 0.0)
        nc.vector.memset(w_planes[:].bitcast(I32), 0)
        make_identity(nc, ident_f32[:])
        make_identity(nc, ident_bf16[:])

        piece_cols = PIECE_PASSES * K_PASS
        x_pieces = []
        for i in range(X_PIECES):
            x_piece = x_pool.tile([P, piece_cols], BF16, name="x_piece%d" % i, bufs=1)
            nc.sync.dma_start(out=x_piece[:], in_=x[:, i * piece_cols : (i + 1) * piece_cols])
            x_pieces.append(x_piece)

        bias_blocks = GROUPS * GOUT // BANK
        nc.scalar.dma_start(
            out=bias_rows[0:bias_blocks, :], in_=b.rearrange("g (a c) -> (g a) c", c=BANK)
        )
        nc.scalar.dma_start(out=bias_rows[bias_blocks : bias_blocks + GROUPS, 0:4], in_=p)
        nc.scalar.dma_start(
            out=bias_rows[bias_blocks : bias_blocks + GROUPS, Q_COLUMN : Q_COLUMN + 3], in_=q
        )

        for j in range(PASSES // PLANES_PER_TILE):
            for quad in range(4):
                nc.gpsimd.dma_start(
                    out=w_planes[32 * quad : 32 * quad + 16, j, :].bitcast(F32),
                    in_=scales_dram[
                        PLANES_PER_TILE * j : PLANES_PER_TILE * (j + 1), 4 * quad : 4 * quad + 4, :
                    ],
                )

        def load_weights(chunk):
            grp, first, width = chunk
            by_pass = []
            g0 = grp * GROUP_PASSES
            for passes in LOADS:
                w_codes = w_pool.tile(
                    [P, passes, width],
                    U32,
                    tag="w_codes%d" % passes,
                    bufs=PREFETCH * sum(1 for n in LOADS if n == passes),
                    align_bytes=64,
                )
                nc.sync.dma_start(
                    out=w_codes[:].bitcast(I32),
                    in_=words_dram[g0 : g0 + passes, :, first : first + width].rearrange(
                        "g p n -> p g n"
                    ),
                )
                for k in range(passes):
                    by_pass.append((w_codes, k))
                g0 += passes
            return by_pass

        chunks = column_chunks()
        w_tiles = {}
        for i in range(PREFETCH):
            w_tiles[i] = load_weights(chunks[i])

        def quantise_piece(i, grouped):
            passes = slice(i * PIECE_PASSES, (i + 1) * PIECE_PASSES)
            nc.vector.quantize_mx(
                out=x_codes[:, passes, :].rearrange("p g n -> p (g n)").bitcast(FP8X4),
                scales=x_planes[:, passes, :].rearrange("p g n -> p (g n)"),
                in_=grouped[:].rearrange("p g n t -> p (g n t)"),
            )

        def spread_bias(j):
            spread = setup_psum.tile([P, BANK], F32, tag="setup")
            nc.tensor.matmul(
                out=spread[:],
                lhsT=ident_bf16[:, j : j + 1].to_broadcast([P, P]),
                rhs=bias_rows[:],
                start=True,
                stop=True,
            )
            copy = nc.vector.tensor_copy if j % 2 == 0 else nc.scalar.copy
            copy(out=bias_all[:, j * BANK : (j + 1) * BANK], in_=spread[:])

        def spread_coefficients():
            spread = setup_psum.tile([P, GROUPS, PQ_COLUMNS], F32, tag="setup")
            for grp in range(GROUPS):
                nc.tensor.matmul(
                    out=spread[:, grp, :],
                    lhsT=ident_bf16[:, bias_blocks + grp : bias_blocks + grp + 1].to_broadcast([P, P]),
                    rhs=bias_rows[:, 0:PQ_COLUMNS],
                    start=True,
                    stop=True,
                )
            nc.vector.tensor_copy(out=pq_f32[:], in_=spread[:])

        piece_blocks = bias_blocks // X_PIECES
        regrouped = []
        for i in range(X_PIECES):
            x_words = x_pieces[i][:].bitcast(F32)
            grouped = x_pool.tile([P, PIECE_PASSES, P, PACK], BF16, align_bytes=64)
            regrouped.append(grouped)
            for half in range(2):
                turned = setup_psum.tile([P, 2, 2, P], F32, tag="setup")
                for g in range(2):
                    w0 = (2 * half + g) * WORDS_PER_PASS
                    for u in range(2):
                        nc.tensor.transpose(
                            turned[:, g, u, :],
                            x_words[:, w0 + u : w0 + WORDS_PER_PASS : 2],
                            ident_f32[:],
                        )
                copy = nc.vector.tensor_copy if half == 0 else nc.scalar.copy
                copy(
                    out=grouped[:, 2 * half : 2 * half + 2, :, :].bitcast(F32),
                    in_=turned[:].rearrange("p g u n -> p g n u"),
                )
            if i > 0:
                quantise_piece(i - 1, regrouped[i - 1])
            for j in range(i * piece_blocks, (i + 1) * piece_blocks):
                spread_bias(j)
        quantise_piece(X_PIECES - 1, regrouped[X_PIECES - 1])

        spread_coefficients()

        def half_slices(width, first=0):
            return [slice(first + h * (width // 2), first + (h + 1) * (width // 2)) for h in range(2)]

        def multiply(i):
            grp, first, width = chunks[i]
            sums = []
            for h in range(2):
                sums.append(acc_psum.tile([P, width // 2], F32, tag="sums", name="sums%d" % h))
            for g_local in range(GROUP_PASSES):
                g = grp * GROUP_PASSES + g_local
                w_codes, place = w_tiles[i][g_local]
                offset = 4 * (g % PLANES_PER_TILE)
                for h in range(2):
                    nc.tensor.matmul_mx(
                        out=sums[h][:],
                        lhsT=x_codes[:, g, :].bitcast(FP8X4),
                        lhsT_scale=x_planes[:, g, :],
                        rhs=w_codes[:, place, half_slices(width)[h]].bitcast(FP8X4),
                        rhs_scale=w_planes[offset:P, g // PLANES_PER_TILE, half_slices(width, first)[h]],
                        start=(g_local == 0),
                        stop=(g_local == GROUP_PASSES - 1),
                    )
            return sums

        def coefficients(grp):
            return (
                [pq_f32[:, grp, c : c + 1] for c in range(4)],
                [pq_f32[:, grp, Q_COLUMN + c : Q_COLUMN + c + 1] for c in range(3)],
            )

        def begin_rational(i, sums):
            grp, first, width = chunks[i]
            (p0, p1, p2, p3), (q0, q1, q2) = coefficients(grp)
            y = work.tile([P, width], F32)
            num = work.tile([P, width], F32)
            den = work.tile([P, width], F32)
            halves = half_slices(width)
            out_halves = half_slices(width, grp * GOUT + first)
            for h in range(2):
                nc.vector.tensor_tensor(
                    out=y[:, halves[h]], in0=sums[h][:], in1=bias_all[:, out_halves[h]], op=ALU.add
                )
            for s in halves:
                nc.scalar.activation(out=den[:, s], in_=y[:, s], func=ACT.Identity, scale=q2, bias=q1)
            for s in halves:
                nc.scalar.activation(out=num[:, s], in_=y[:, s], func=ACT.Identity, scale=p3, bias=p2)
            return y, num, den

        def continue_rational(i, y, num, den):
            grp, first, width = chunks[i]
            (p0, p1, p2, p3), (q0, q1, q2) = coefficients(grp)
            halves = half_slices(width)
            for s in halves:
                nc.vector.tensor_tensor(out=den[:, s], in0=den[:, s], in1=y[:, s], op=ALU.mult)
            for s in halves:
                nc.vector.scalar_tensor_tensor(
                    out=den[:, s], in0=den[:, s], scalar=q0, in1=y[:, s], op0=ALU.add, op1=ALU.mult
                )
            for s in halves:
                nc.scalar.activation(out=den[:, s], in_=den[:, s], func=ACT.Abs)
            for s in halves:
                nc.scalar.activation(
                    out=den[:, s], in_=den[:, s], func=ACT.Abs_reciprocal_sqrt, bias=1.0
                )
            for s in halves:
                nc.scalar.activation(out=den[:, s], in_=den[:, s], func=ACT.Square)
            for s in halves:
                nc.vector.tensor_tensor(out=num[:, s], in0=num[:, s], in1=y[:, s], op=ALU.mult)
            for s in halves:
                nc.vector.scalar_tensor_tensor(
                    out=num[:, s], in0=num[:, s], scalar=p1, in1=y[:, s], op0=ALU.add, op1=ALU.mult
                )

        def finish_rational(i, num, den):
            grp, first, width = chunks[i]
            (p0, p1, p2, p3), (q0, q1, q2) = coefficients(grp)
            halves = half_slices(width)
            out_halves = half_slices(width, grp * GOUT + first)
            for h in range(2):
                nc.vector.scalar_tensor_tensor(
                    out=result[:, out_halves[h]],
                    in0=num[:, halves[h]],
                    scalar=p0,
                    in1=den[:, halves[h]],
                    op0=ALU.add,
                    op1=ALU.mult,
                )

        waiting = None
        for i in range(len(chunks)):
            sums = multiply(i)
            if i + PREFETCH < len(chunks):
                w_tiles[i + PREFETCH] = load_weights(chunks[i + PREFETCH])
            y, num, den = begin_rational(i, sums)
            if waiting is not None:
                finish_rational(*waiting)
            continue_rational(i, y, num, den)
            waiting = (i, num, den)
        finish_rational(*waiting)

        for grp, first, width in chunks:
            cols = slice(grp * GOUT + first, grp * GOUT + first + width)
            nc.sync.dma_start(out=out[:, cols], in_=result[:, cols])
